import numpy as np
import ml_dtypes


def mxq(x, axis, fmt="e4m3"):
    dtype, down = {"e4m3": (ml_dtypes.float8_e4m3fn, 7), "e5m2": (ml_dtypes.float8_e5m2, 14)}[fmt]
    v = np.moveaxis(np.asarray(x, np.float32).astype(ml_dtypes.bfloat16).astype(np.float64), axis, -1)
    blocks = v.reshape(v.shape[:-1] + (-1, 32))
    amax = np.abs(blocks).max(-1, keepdims=True)
    byte = np.maximum(np.where(amax > 0, np.frexp(amax)[1] - 1 + 127, 0) - down, 1)
    scale = np.exp2(byte - 127.0)
    codes = (blocks / scale).astype(np.float32).astype(dtype).astype(np.float64)
    return np.moveaxis((codes * scale).reshape(v.shape), -1, axis)


WIDE = False


def mx_kscale(k):
    if not WIDE:
        return np.ones(k)
    levels = np.array([10, -10, 5, -5, 0])
    if k % 512:
        return np.exp2(np.random.permutation(np.resize(levels, k // 32))).repeat(32)
    a = np.empty((k // 512, 16))
    for p in range(k // 512):
        a[p, :8] = np.random.permutation(np.resize(levels, 8))
        for g in range(8):
            far = levels[np.abs(levels - a[p, g]) >= 10]
            a[p, g + 8] = far[np.random.randint(len(far))]
    return np.exp2(a.ravel()).repeat(32)


BF16 = ml_dtypes.bfloat16


def bf(x):
    return np.asarray(x, np.float32).astype(BF16)


def f64(x):
    return np.asarray(x).astype(np.float64)


B, S, D, H, QK = 8, 1024, 1024, 64, 128
EPS = 1e-5
R = np.sqrt(0.1 * S / np.sqrt(QK))


def silu(a):
    return a / (1.0 + np.exp(-a))


def setup_inputs():
    s = mx_kscale(D)
    return {
        "x": bf(np.random.standard_normal((B, S, D)) + 0.5 * np.random.standard_normal((B, S, 1))),
        "ln_w": bf((1.0 + 0.1 * np.random.standard_normal(D)) * s),
        "ln_b": bf(0.1 * np.random.standard_normal(D) * s),
        "W_hidden": bf(np.random.standard_normal((2 * H, D)) / np.sqrt(D) / s),
        "b_hidden": bf(0.1 * np.random.standard_normal(2 * H)),
        "W_qk": bf(np.random.standard_normal((QK, D)) / np.sqrt(D) / s),
        "b_qk": bf(0.1 * np.random.standard_normal(QK)),
        "gamma": bf(np.random.standard_normal((2, QK)) * R / 0.6),
        "beta": bf(np.random.standard_normal((2, QK)) * R * 0.3),
    }


def reference(x, ln_w, ln_b, W_hidden, b_hidden, W_qk, b_qk, gamma, beta):
    x = f64(x)
    mu = x.mean(-1, keepdims=True)
    var = np.square(x - mu).mean(-1, keepdims=True)
    normed = (x - mu) / np.sqrt(var + EPS) * f64(ln_w) + f64(ln_b)
    nq = mxq(normed, 2, "e4m3")
    hg = silu((nq @ mxq(f64(W_hidden), 1, "e4m3").T) + f64(b_hidden))
    v, gate = hg[..., :H], hg[..., H:]
    Z = silu((nq @ mxq(f64(W_qk), 1, "e4m3").T) + f64(b_qk))
    gamma, beta = f64(gamma), f64(beta)
    q = Z * gamma[0] + beta[0]
    k = Z * gamma[1] + beta[1]
    return v, gate, q, k

@@ -1,0 +1,341 @@
+from contextlib import ExitStack
+
+import concourse.mybir as mybir
+from concourse.masks import make_identity
+
+F32 = mybir.dt.float32
+BF16 = mybir.dt.bfloat16
+U32 = mybir.dt.uint32
+U8 = mybir.dt.uint8
+FP8X4 = mybir.dt.float8_e4m3fn_x4
+ALU = mybir.AluOpType
+ACT = mybir.ActivationFunctionType
+
+P = 128
+D = 1024
+ROWS = 8192
+JT = 4
+SUP = P * JT
+NSUP = ROWS // SUP
+KB = D // P
+EPS = 1e-5
+FLOPS = 2 * ROWS * D * 256
+
+B_ENGINE = ("g", "g", "g", "s")
+
+
+def tile_gau_pb_t_kernel(
+    tc, x, ln_w, ln_b, W_hidden, b_hidden, W_qk, b_qk, gamma, beta, out_0, out_1, out_2, out_3
+):
+    nc = tc.nc
+    xf = x.flatten_outer_dims()
+    outs = {
+        "v": out_0.flatten_outer_dims(),
+        "g": out_1.flatten_outer_dims(),
+        "q": out_2.flatten_outer_dims(),
+        "k": out_3.flatten_outer_dims(),
+    }
+
+    with ExitStack() as ctx:
+        ctx.enter_context(tc.manual_schedule())
+        keep = ctx.enter_context(tc.tile_pool(name="keep", bufs=1))
+        xpool = ctx.enter_context(tc.tile_pool(name="xpool", bufs=4))
+        small = ctx.enter_context(tc.tile_pool(name="small", bufs=4))
+        ypool = ctx.enter_context(tc.tile_pool(name="ypool", bufs=2))
+        upool = ctx.enter_context(tc.tile_pool(name="upool", bufs=2))
+        gpool = ctx.enter_context(tc.tile_pool(name="gpool", bufs=2))
+        cpool = ctx.enter_context(tc.tile_pool(name="cpool", bufs=2))
+        epool = ctx.enter_context(tc.tile_pool(name="epool", bufs=2))
+        opool = ctx.enter_context(tc.tile_pool(name="opool", bufs=2))
+        ps_in = ctx.enter_context(tc.psum_pool(name="ps_in", bufs=3))
+        ps_acc = ctx.enter_context(tc.psum_pool(name="ps_acc", bufs=1))
+        ps_out = ctx.enter_context(tc.psum_pool(name="ps_out", bufs=3))
+
+        T = {}
+
+        def valid(s):
+            return 0 <= s < NSUP
+
+        ident = keep.tile([P, P], F32, name="ident")
+        make_identity(nc, ident[:])
+        mhalf = keep.tile([P, JT], F32, name="mhalf")
+        nc.vector.memset(mhalf[:], -0.5)
+        cst_b = keep.tile([P, P], BF16, name="cst_b")
+        nc.vector.memset(cst_b[:], 0.0)
+        for r0, vec in ((0, ln_w), (8, ln_b)):
+            for g in range(2):
+                nc.scalar.dma_start(
+                    out=cst_b[r0 + 4 * g : r0 + 4 * g + 4, :].rearrange("t (m r) -> t m r", r=8),
+                    in_=vec[512 * g : 512 * (g + 1)].rearrange("(m t r) -> t m r", t=4, r=8),
+                )
+        nc.scalar.dma_start(out=cst_b[16:17, :], in_=b_hidden.rearrange("(a b) -> a b", b=P))
+        nc.scalar.dma_start(out=cst_b[17:18, :], in_=b_qk.rearrange("(a b) -> a b", b=P))
+        nc.scalar.dma_start(out=cst_b[18:20, :], in_=gamma)
+        nc.scalar.dma_start(out=cst_b[20:22, :], in_=beta)
+        wbs = []
+        for h, W in enumerate((W_hidden, W_qk)):
+            wb = keep.tile([P, D], BF16, name="wb%d" % h)
+            nc.scalar.dma_start(out=wb[:], in_=W)
+            wbs.append(wb)
+        cols = keep.tile([P, 32], F32, name="cols")
+        wgrp = keep.tile([P, 4, P, 4], BF16, name="wgrp", align_bytes=64)
+        wcodes = keep.tile([P, 4, P], U32, name="wcodes", align_bytes=64)
+        wsc = keep.tile([P, 4, P], U8, name="wsc", align_bytes=64)
+
+        def prep_consts():
+            cst_f = keep.tile([P, P], F32, name="cst_f")
+            nc.scalar.copy(out=cst_f[:], in_=cst_b[:])
+            tpc = ps_in.tile([P, 512], F32, tag="tin", name="tpc")
+            nc.tensor.transpose(tpc[:, 0:P], cst_f[:], ident[:])
+            nc.scalar.copy(out=cols[:, 0:22], in_=tpc[:, 0:22])
+
+        def prep_weights():
+            for h in range(2):
+                wf = keep.tile([P, D], F32, name="wf%d" % h)
+                nc.scalar.copy(
+                    out=wf[:].rearrange("p (t m r) -> p t m r", t=4, r=8),
+                    in_=wbs[h][:].rearrange("p (m t r) -> p t m r", t=4, r=8),
+                )
+                for g in range(2):
+                    tpw = ps_in.tile([P, 512], F32, tag="tin", name="tpw")
+                    for t in range(4):
+                        c0 = 256 * t + P * g
+                        nc.tensor.transpose(tpw[:, P * t : P * (t + 1)], wf[:, c0 : c0 + P], ident[:])
+                    nc.scalar.copy(
+                        out=wgrp[:, 2 * h + g, :, :], in_=tpw[:].rearrange("p (t o) -> p o t", t=4)
+                    )
+
+        def quant_weights():
+            nc.vector.quantize_mx(
+                out=wcodes[:].rearrange("p a o -> p (a o)").bitcast(FP8X4),
+                scales=wsc[:].rearrange("p a o -> p (a o)"),
+                in_=wgrp[:].rearrange("p a o t -> p (a o t)"),
+            )
+
+        def load(s):
+            if not valid(s):
+                return
+            xs = xpool.tile([P, JT, D], BF16, name="xs")
+            T["xs", s] = xs
+            src = xf[SUP * s : SUP * (s + 1), :].rearrange("(p j) k -> p j k", j=JT)
+            if s == 0:
+                for j in range(JT):
+                    nc.sync.dma_start(out=xs[:, j, :], in_=src[:, j, :])
+            else:
+                nc.sync.dma_start(out=xs[:], in_=src)
+
+        def stats(s):
+            if not valid(s):
+                return
+            xs = T["xs", s]
+            st = small.tile([P, JT, 2, 6], F32, name="st")
+            mv = small.tile([P, JT, 2], F32, name="mv")
+            for j in range(JT):
+                for c in range(2):
+                    nc.vector.bn_stats(out=st[:, j, c, :], in_=xs[:, j, 512 * c : 512 * (c + 1)])
+                nc.vector.bn_aggr(out=mv[:, j, :], in_=st[:, j, :, :].rearrange("p c v -> p (c v)"))
+            ve = small.tile([P, JT], F32, name="ve")
+            nc.vector.tensor_scalar_add(out=ve[:], in0=mv[:, :, 1], scalar1=EPS)
+            negmu = small.tile([P, JT], F32, name="negmu")
+            nc.vector.tensor_scalar_mul(out=negmu[:], in0=mv[:, :, 0], scalar1=-1.0)
+            T["ve", s] = ve
+            T["negmu", s] = negmu
+
+        def rstd_stage(s):
+            if not valid(s):
+                return
+            rstd = small.tile([P, JT], F32, name="rstd")
+            nc.gpsimd.tensor_tensor(out=rstd[:], in0=T["ve", s][:], in1=mhalf[:], op=ALU.pow)
+            T["rstd", s] = rstd
+
+        def gate(s):
+            if not valid(s):
+                return
+            late = small.tile([P, JT], F32, name="late")
+            nc.vector.tensor_copy(out=late[:], in_=T["negmu", s][:])
+            T["late", s] = late
+
+        def nmr_stage(s):
+            if not valid(s):
+                return
+            nmr = small.tile([P, JT], F32, name="nmr")
+            nc.gpsimd.tensor_tensor(out=nmr[:], in0=T["late", s][:], in1=T["rstd", s][:], op=ALU.mult)
+            T["nmr", s] = nmr
+
+        def norm(s, eng):
+            if not valid(s):
+                return
+            if ("y", s) not in T:
+                T["y", s] = ypool.tile([P, JT, D], F32, name="y")
+            y = T["y", s]
+            xs = T["xs", s]
+            rstd = T["rstd", s]
+            for j in range(JT):
+                if B_ENGINE[j] != eng:
+                    continue
+                y_j = y[:, j, :].rearrange("p (t m r) -> p t m r", t=4, r=8)
+                x_j = xs[:, j, :].rearrange("p (m t r) -> p t m r", t=4, r=8)
+                if eng == "g":
+                    nc.gpsimd.tensor_scalar(
+                        out=y_j, in0=x_j,
+                        scalar1=T["late", s][:, j : j + 1], scalar2=rstd[:, j : j + 1],
+                        op0=ALU.add, op1=ALU.mult,
+                    )
+                elif eng == "s":
+                    nc.scalar.activation(
+                        out=y_j, in_=x_j, func=ACT.Identity,
+                        bias=T["nmr", s][:, j : j + 1], scale=rstd[:, j : j + 1],
+                    )
+                else:
+                    nc.vector.tensor_scalar(
+                        out=y_j, in0=x_j,
+                        scalar1=T["negmu", s][:, j : j + 1], scalar2=rstd[:, j : j + 1],
+                        op0=ALU.add, op1=ALU.mult,
+                    )
+
+        def t1c(s):
+            if not valid(s):
+                return
+            y = T["y", s]
+            u = upool.tile([P, KB, SUP], BF16, name="u")
+            T["u", s] = u
+            for kb in range(KB):
+                tp = ps_in.tile([P, 512], F32, tag="tin", name="tp")
+                c0 = 256 * (kb % 4) + P * (kb // 4)
+                for j in range(JT):
+                    nc.tensor.transpose(tp[:, P * j : P * (j + 1)], y[:, j, c0 : c0 + P], ident[:])
+                nc.scalar.activation(
+                    out=u[:, kb, :], in_=tp[:], func=ACT.Identity,
+                    bias=cols[:, 8 + kb : 9 + kb], scale=cols[:, kb : kb + 1],
+                )
+
+        def regroup_quant(s):
+            if not valid(s):
+                return
+            u = T["u", s]
+            codes = cpool.tile([P, 2, SUP], U32, name="codes", align_bytes=64)
+            sc = cpool.tile([P, 2, SUP], U8, name="sc", align_bytes=64)
+            T["codes", s] = codes
+            T["sc", s] = sc
+            grps = []
+            for g in range(2):
+                grp = gpool.tile([P, SUP, 4], BF16, name="grp%d" % g, align_bytes=64)
+                nc.vector.tensor_copy(
+                    out=grp[:].rearrange("p (c i) t -> p c t i", i=4),
+                    in_=u[:, 4 * g : 4 * g + 4, :].rearrange("p t (c i) -> p c t i", i=4),
+                )
+                grps.append(grp)
+            for g in range(2):
+                nc.vector.quantize_mx(
+                    out=codes[:, g, :].bitcast(FP8X4),
+                    scales=sc[:, g, :],
+                    in_=grps[g][:].rearrange("p c t -> p (c t)"),
+                )
+
+        def mx(s):
+            if not valid(s):
+                return
+            codes = T["codes", s]
+            sc = T["sc", s]
+            for h in range(2):
+                acc = ps_acc.tile([P, SUP], F32, name="acc%d" % h)
+                T["acc%d" % h, s] = acc
+                for g in range(2):
+                    nc.tensor.matmul_mx(
+                        out=acc[:],
+                        lhsT=wcodes[:, 2 * h + g, :].bitcast(FP8X4),
+                        lhsT_scale=wsc[:, 2 * h + g, :],
+                        rhs=codes[:, g, :].bitcast(FP8X4),
+                        rhs_scale=sc[:, g, :],
+                        start=(g == 0),
+                        stop=(g == 1),
+                    )
+
+        def silu(s):
+            if not valid(s):
+                return
+            hgT = epool.tile([P, SUP], F32, name="hgT")
+            nc.scalar.activation(out=hgT[:], in_=T["acc0", s][:], func=ACT.Silu, bias=cols[:, 16:17], scale=1.0)
+            zT = epool.tile([P, SUP], F32, name="zT")
+            nc.scalar.activation(out=zT[:], in_=T["acc1", s][:], func=ACT.Silu, bias=cols[:, 17:18], scale=1.0)
+            T["hg", s] = hgT
+            T["z", s] = zT
+
+        def qk(s):
+            if not valid(s):
+                return
+            zT = T["z", s]
+            for i, nm in enumerate(("q", "k")):
+                t = epool.tile([P, SUP], F32, name=nm + "T")
+                nc.scalar.activation(
+                    out=t[:], in_=zT[:], func=ACT.Identity,
+                    bias=cols[:, 20 + i : 21 + i], scale=cols[:, 18 + i : 19 + i],
+                )
+                T[nm, s] = t
+
+        def t2(s, nm):
+            if not valid(s):
+                return
+            src = T[nm, s]
+            to = ps_out.tile([P, 512], F32, tag="tout", name="to_" + nm)
+            T["to_" + nm, s] = to
+            for j in range(JT):
+                nc.tensor.transpose(to[:, P * j : P * (j + 1)], src[:, P * j : P * (j + 1)], ident[:])
+
+        def evac(s, nm, eng="s"):
+            if not valid(s):
+                return
+            to = T["to_" + nm, s]
+            if nm == "hg":
+                dst = opool.tile([P, 2, JT, 64], F32, name="o_hg")
+                o_ap = dst[:]
+                i_ap = to[:].rearrange("p (j h o) -> p h j o", j=JT, h=2)
+            else:
+                dst = opool.tile([P, JT, P], F32, name="o_" + nm)
+                o_ap = dst[:].rearrange("p j o -> p (j o)")
+                i_ap = to[:]
+            T["o_" + nm, s] = dst
+            if eng == "s":
+                nc.scalar.copy(out=o_ap, in_=i_ap)
+            else:
+                nc.vector.tensor_copy(out=o_ap, in_=i_ap)
+
+        def store(s, nm):
+            if not valid(s):
+                return
+            rows = slice(SUP * s, SUP * (s + 1))
+            if nm == "hg":
+                o = T["o_hg", s]
+                nc.sync.dma_start(out=outs["v"][rows, :].rearrange("(p j) o -> p j o", j=JT), in_=o[:, 0, :, :])
+                nc.sync.dma_start(out=outs["g"][rows, :].rearrange("(p j) o -> p j o", j=JT), in_=o[:, 1, :, :])
+            else:
+                nc.sync.dma_start(out=outs[nm][rows, :].rearrange("(p j) o -> p j o", j=JT), in_=T["o_" + nm, s][:])
+
+        load(0)
+        load(1)
+        prep_consts()
+        prep_weights()
+        for i in range(NSUP + 5):
+            load(i + 2)
+            stats(i)
+            if i == 1:
+                quant_weights()
+            nmr_stage(i - 1)
+            norm(i - 1, "g")
+            rstd_stage(i)
+            norm(i - 1, "s")
+            mx(i - 3)
+            t2(i - 4, "q")
+            t2(i - 4, "k")
+            silu(i - 3)
+            t2(i - 3, "hg")
+            evac(i - 4, "q")
+            evac(i - 4, "k")
+            store(i - 4, "q")
+            store(i - 4, "k")
+            evac(i - 3, "hg")
+            store(i - 3, "hg")
+            t1c(i - 1)
+            qk(i - 3)
+            regroup_quant(i - 2)
+            gate(i)

@@ -14,14 +14,27 @@ ACT = mybir.ActivationFunctionType
 P = 128
 D = 1024
 ROWS = 8192
-JT = 4
-SUP = P * JT
-NSUP = ROWS // SUP
 KB = D // P
 EPS = 1e-5
 FLOPS = 2 * ROWS * D * 256
 
-B_ENGINE = ("g", "g", "g", "s")
+WIDTHS = [1, 1, 2] + [4] * 14 + [2, 1, 1]
+FIRST = [sum(WIDTHS[:s]) for s in range(len(WIDTHS))]
+NS = len(WIDTHS)
+AHEAD = 4
+LEAD = 1
+GATES = 3
+
+
+def owners(s):
+    w = WIDTHS[s]
+    if s >= NS - 2:
+        return "v" * w
+    return {1: "s", 2: "gs", 4: "gggs"}[w]
+
+
+def vshare(s):
+    return 3 if s >= NS - 4 else 0
 
 
 def tile_gau_pb_t_kernel(
@@ -39,7 +52,7 @@ def tile_gau_pb_t_kernel(
     with ExitStack() as ctx:
         ctx.enter_context(tc.manual_schedule())
         keep = ctx.enter_context(tc.tile_pool(name="keep", bufs=1))
-        xpool = ctx.enter_context(tc.tile_pool(name="xpool", bufs=4))
+        xpool = ctx.enter_context(tc.tile_pool(name="xpool", bufs=7))
         small = ctx.enter_context(tc.tile_pool(name="small", bufs=4))
         ypool = ctx.enter_context(tc.tile_pool(name="ypool", bufs=2))
         upool = ctx.enter_context(tc.tile_pool(name="upool", bufs=2))
@@ -54,55 +67,68 @@ def tile_gau_pb_t_kernel(
         T = {}
 
         def valid(s):
-            return 0 <= s < NSUP
+            return 0 <= s < NS
 
+        warm = keep.tile([P, 1], F32, name="warm")
+        nc.vector.memset(warm[:], 0.0)
+        cst_b = keep.tile([P, 640], BF16, name="cst_b")
+        nc.vector.memset(cst_b[:], 0.0)
+        cst_p = keep.tile([P, 640], BF16, name="cst_p")
+        mhalf = keep.tile([P, 4], F32, name="mhalf")
+        nc.vector.memset(mhalf[:], -0.5)
+        nc.scalar.activation(out=warm[:], in_=warm[:], func=ACT.Silu)
         ident = keep.tile([P, P], F32, name="ident")
         make_identity(nc, ident[:])
-        mhalf = keep.tile([P, JT], F32, name="mhalf")
-        nc.vector.memset(mhalf[:], -0.5)
-        cst_b = keep.tile([P, P], BF16, name="cst_b")
-        nc.vector.memset(cst_b[:], 0.0)
-        for r0, vec in ((0, ln_w), (8, ln_b)):
-            for g in range(2):
-                nc.scalar.dma_start(
-                    out=cst_b[r0 + 4 * g : r0 + 4 * g + 4, :].rearrange("t (m r) -> t m r", r=8),
-                    in_=vec[512 * g : 512 * (g + 1)].rearrange("(m t r) -> t m r", t=4, r=8),
-                )
-        nc.scalar.dma_start(out=cst_b[16:17, :], in_=b_hidden.rearrange("(a b) -> a b", b=P))
-        nc.scalar.dma_start(out=cst_b[17:18, :], in_=b_qk.rearrange("(a b) -> a b", b=P))
-        nc.scalar.dma_start(out=cst_b[18:20, :], in_=gamma)
-        nc.scalar.dma_start(out=cst_b[20:22, :], in_=beta)
-        wbs = []
-        for h, W in enumerate((W_hidden, W_qk)):
-            wb = keep.tile([P, D], BF16, name="wb%d" % h)
-            nc.scalar.dma_start(out=wb[:], in_=W)
-            wbs.append(wb)
+        ident_b = keep.tile([P, P], BF16, name="ident_b")
+        make_identity(nc, ident_b[:])
         cols = keep.tile([P, 32], F32, name="cols")
+        wbs = [keep.tile([P, D], BF16, name="wb%d" % h) for h in range(2)]
+        wps = [keep.tile([P, D], BF16, name="wp%d" % h) for h in range(2)]
         wgrp = keep.tile([P, 4, P, 4], BF16, name="wgrp", align_bytes=64)
         wcodes = keep.tile([P, 4, P], U32, name="wcodes", align_bytes=64)
         wsc = keep.tile([P, 4, P], U8, name="wsc", align_bytes=64)
 
+        def load_consts():
+            for r0, vec in ((0, ln_w), (2, ln_b)):
+                nc.sync.dma_start(out=cst_b[r0 : r0 + 2, 0:512], in_=vec.rearrange("(g f) -> g f", f=512))
+            nc.sync.dma_start(out=cst_b[0:1, 512:640], in_=b_hidden.rearrange("(a b) -> a b", b=P))
+            nc.sync.dma_start(out=cst_b[1:2, 512:640], in_=b_qk.rearrange("(a b) -> a b", b=P))
+            nc.sync.dma_start(out=cst_b[2:4, 512:640], in_=gamma)
+            nc.sync.dma_start(out=cst_b[4:6, 512:640], in_=beta)
+
+        def load_weights():
+            for h, W in enumerate((W_hidden, W_qk)):
+                nc.sync.dma_start(out=wbs[h][:], in_=W)
+
         def prep_consts():
-            cst_f = keep.tile([P, P], F32, name="cst_f")
-            nc.scalar.copy(out=cst_f[:], in_=cst_b[:])
-            tpc = ps_in.tile([P, 512], F32, tag="tin", name="tpc")
-            nc.tensor.transpose(tpc[:, 0:P], cst_f[:], ident[:])
-            nc.scalar.copy(out=cols[:, 0:22], in_=tpc[:, 0:22])
+            nc.scalar.copy(
+                out=cst_p[:, 0:512].rearrange("p (t m r) -> p t m r", t=4, r=8),
+                in_=cst_b[:, 0:512].rearrange("p (m t r) -> p t m r", t=4, r=8),
+            )
+            tpc = ps_in.tile([P, 1024], BF16, tag="tin", name="tpc")
+            for t in range(4):
+                nc.tensor.transpose(tpc[:, P * t : P * (t + 1)], cst_p[:, P * t : P * (t + 1)], ident_b[:])
+            nc.tensor.transpose(tpc[:, 512:640], cst_b[:, 512:640], ident_b[:])
+            nc.scalar.copy(
+                out=cols[:, 0:16].rearrange("p (v t) -> p v t", t=4),
+                in_=tpc[:, 0:512].rearrange("p (t c) -> p c t", t=4)[:, 0:4, :],
+            )
+            nc.scalar.copy(out=cols[:, 16:22], in_=tpc[:, 512:518])
 
         def prep_weights():
             for h in range(2):
-                wf = keep.tile([P, D], F32, name="wf%d" % h)
                 nc.scalar.copy(
-                    out=wf[:].rearrange("p (t m r) -> p t m r", t=4, r=8),
+                    out=wps[h][:].rearrange("p (t m r) -> p t m r", t=4, r=8),
                     in_=wbs[h][:].rearrange("p (m t r) -> p t m r", t=4, r=8),
                 )
+            for h in range(2):
                 for g in range(2):
-                    tpw = ps_in.tile([P, 512], F32, tag="tin", name="tpw")
+                    tpw = ps_in.tile([P, 1024], BF16, tag="tin", name="tpw")
                     for t in range(4):
                         c0 = 256 * t + P * g
-                        nc.tensor.transpose(tpw[:, P * t : P * (t + 1)], wf[:, c0 : c0 + P], ident[:])
+                        nc.tensor.transpose(tpw[:, P * t : P * (t + 1)], wps[h][:, c0 : c0 + P], ident_b[:])
                     nc.scalar.copy(
-                        out=wgrp[:, 2 * h + g, :, :], in_=tpw[:].rearrange("p (t o) -> p o t", t=4)
+                        out=wgrp[:, 2 * h + g, :, :], in_=tpw[:, 0:512].rearrange("p (t o) -> p o t", t=4)
                     )
 
         def quant_weights():
@@ -112,82 +138,88 @@ def tile_gau_pb_t_kernel(
                 in_=wgrp[:].rearrange("p a o t -> p (a o t)"),
             )
 
+        def rows_of(s):
+            return slice(P * FIRST[s], P * (FIRST[s] + WIDTHS[s]))
+
         def load(s):
             if not valid(s):
                 return
-            xs = xpool.tile([P, JT, D], BF16, name="xs")
+            w = WIDTHS[s]
+            xs = xpool.tile([P, 4, D], BF16, name="xs")
             T["xs", s] = xs
-            src = xf[SUP * s : SUP * (s + 1), :].rearrange("(p j) k -> p j k", j=JT)
-            if s == 0:
-                for j in range(JT):
-                    nc.sync.dma_start(out=xs[:, j, :], in_=src[:, j, :])
-            else:
-                nc.sync.dma_start(out=xs[:], in_=src)
+            nc.sync.dma_start(out=xs[:, 0:w, :], in_=xf[rows_of(s), :].rearrange("(p j) k -> p j k", j=w))
 
         def stats(s):
             if not valid(s):
                 return
+            w = WIDTHS[s]
             xs = T["xs", s]
-            st = small.tile([P, JT, 2, 6], F32, name="st")
-            mv = small.tile([P, JT, 2], F32, name="mv")
-            for j in range(JT):
+            st = small.tile([P, 4, 2, 6], F32, name="st")
+            mv = small.tile([P, 4, 2], F32, name="mv")
+            T["st", s] = st
+            T["mv", s] = mv
+            for j in range(w):
                 for c in range(2):
                     nc.vector.bn_stats(out=st[:, j, c, :], in_=xs[:, j, 512 * c : 512 * (c + 1)])
-                nc.vector.bn_aggr(out=mv[:, j, :], in_=st[:, j, :, :].rearrange("p c v -> p (c v)"))
-            ve = small.tile([P, JT], F32, name="ve")
-            nc.vector.tensor_scalar_add(out=ve[:], in0=mv[:, :, 1], scalar1=EPS)
-            negmu = small.tile([P, JT], F32, name="negmu")
-            nc.vector.tensor_scalar_mul(out=negmu[:], in0=mv[:, :, 0], scalar1=-1.0)
+                if j > 0:
+                    aggr(s, j - 1)
+
+        def aggr(s, j):
+            nc.vector.bn_aggr(
+                out=T["mv", s][:, j, :], in_=T["st", s][:, j, :, :].rearrange("p c v -> p (c v)")
+            )
+
+        def last_aggr(s):
+            if valid(s):
+                aggr(s, WIDTHS[s] - 1)
+
+        def gate(s):
+            if not valid(s):
+                return
+            w = WIDTHS[s]
+            mv = T["mv", s]
+            ve = small.tile([P, 4], F32, name="ve")
+            nc.vector.tensor_scalar_add(out=ve[:, 0:w], in0=mv[:, 0:w, 1], scalar1=EPS)
+            negmu = small.tile([P, 4], F32, name="negmu")
+            nc.vector.tensor_scalar_mul(out=negmu[:, 0:w], in0=mv[:, 0:w, 0], scalar1=-1.0)
             T["ve", s] = ve
             T["negmu", s] = negmu
 
         def rstd_stage(s):
             if not valid(s):
                 return
-            rstd = small.tile([P, JT], F32, name="rstd")
-            nc.gpsimd.tensor_tensor(out=rstd[:], in0=T["ve", s][:], in1=mhalf[:], op=ALU.pow)
+            w = WIDTHS[s]
+            rstd = small.tile([P, 4], F32, name="rstd")
+            nc.gpsimd.tensor_tensor(out=rstd[:, 0:w], in0=T["ve", s][:, 0:w], in1=mhalf[:, 0:w], op=ALU.pow)
             T["rstd", s] = rstd
-
-        def gate(s):
-            if not valid(s):
-                return
-            late = small.tile([P, JT], F32, name="late")
-            nc.vector.tensor_copy(out=late[:], in_=T["negmu", s][:])
-            T["late", s] = late
-
-        def nmr_stage(s):
-            if not valid(s):
-                return
-            nmr = small.tile([P, JT], F32, name="nmr")
-            nc.gpsimd.tensor_tensor(out=nmr[:], in0=T["late", s][:], in1=T["rstd", s][:], op=ALU.mult)
-            T["nmr", s] = nmr
+            if "s" in owners(s):
+                nmr = small.tile([P, 4], F32, name="nmr")
+                nc.gpsimd.tensor_tensor(
+                    out=nmr[:, 0:w], in0=T["negmu", s][:, 0:w], in1=rstd[:, 0:w], op=ALU.mult
+                )
+                T["nmr", s] = nmr
 
         def norm(s, eng):
             if not valid(s):
                 return
             if ("y", s) not in T:
-                T["y", s] = ypool.tile([P, JT, D], F32, name="y")
+                T["y", s] = ypool.tile([P, 4, D], F32, name="y")
             y = T["y", s]
             xs = T["xs", s]
             rstd = T["rstd", s]
-            for j in range(JT):
-                if B_ENGINE[j] != eng:
+            for j in range(WIDTHS[s]):
+                if owners(s)[j] != eng:
                     continue
                 y_j = y[:, j, :].rearrange("p (t m r) -> p t m r", t=4, r=8)
                 x_j = xs[:, j, :].rearrange("p (m t r) -> p t m r", t=4, r=8)
-                if eng == "g":
-                    nc.gpsimd.tensor_scalar(
-                        out=y_j, in0=x_j,
-                        scalar1=T["late", s][:, j : j + 1], scalar2=rstd[:, j : j + 1],
-                        op0=ALU.add, op1=ALU.mult,
-                    )
-                elif eng == "s":
+                if eng == "s":
                     nc.scalar.activation(
                         out=y_j, in_=x_j, func=ACT.Identity,
                         bias=T["nmr", s][:, j : j + 1], scale=rstd[:, j : j + 1],
                     )
                 else:
-                    nc.vector.tensor_scalar(
+                    e = nc.gpsimd if eng == "g" else nc.vector
+                    e.tensor_scalar(
                         out=y_j, in0=x_j,
                         scalar1=T["negmu", s][:, j : j + 1], scalar2=rstd[:, j : j + 1],
                         op0=ALU.add, op1=ALU.mult,
@@ -196,57 +228,73 @@ def tile_gau_pb_t_kernel(
         def t1c(s):
             if not valid(s):
                 return
+            w = WIDTHS[s]
+            n = P * w
             y = T["y", s]
-            u = upool.tile([P, KB, SUP], BF16, name="u")
+            u = upool.tile([P, KB, 512], BF16, name="u")
             T["u", s] = u
             for kb in range(KB):
                 tp = ps_in.tile([P, 512], F32, tag="tin", name="tp")
+                T["tp%d" % kb, s] = tp
                 c0 = 256 * (kb % 4) + P * (kb // 4)
-                for j in range(JT):
+                for j in range(w):
                     nc.tensor.transpose(tp[:, P * j : P * (j + 1)], y[:, j, c0 : c0 + P], ident[:])
-                nc.scalar.activation(
-                    out=u[:, kb, :], in_=tp[:], func=ACT.Identity,
-                    bias=cols[:, 8 + kb : 9 + kb], scale=cols[:, kb : kb + 1],
+                if kb < KB - vshare(s):
+                    nc.scalar.activation(
+                        out=u[:, kb, 0:n], in_=tp[:, 0:n], func=ACT.Identity,
+                        bias=cols[:, 8 + kb : 9 + kb], scale=cols[:, kb : kb + 1],
+                    )
+
+        def evac_v(s):
+            if not valid(s):
+                return
+            n = P * WIDTHS[s]
+            for kb in range(KB - vshare(s), KB):
+                nc.vector.tensor_scalar(
+                    out=T["u", s][:, kb, 0:n], in0=T["tp%d" % kb, s][:, 0:n],
+                    scalar1=cols[:, kb : kb + 1], scalar2=cols[:, 8 + kb : 9 + kb], op0=ALU.mult, op1=ALU.add,
                 )
 
         def regroup_quant(s):
             if not valid(s):
                 return
+            n = P * WIDTHS[s]
             u = T["u", s]
-            codes = cpool.tile([P, 2, SUP], U32, name="codes", align_bytes=64)
-            sc = cpool.tile([P, 2, SUP], U8, name="sc", align_bytes=64)
+            codes = cpool.tile([P, 2, 512], U32, name="codes", align_bytes=64)
+            sc = cpool.tile([P, 2, 512], U8, name="sc", align_bytes=64)
             T["codes", s] = codes
             T["sc", s] = sc
             grps = []
             for g in range(2):
-                grp = gpool.tile([P, SUP, 4], BF16, name="grp%d" % g, align_bytes=64)
+                grp = gpool.tile([P, 512, 4], BF16, name="grp%d" % g, align_bytes=64)
                 nc.vector.tensor_copy(
-                    out=grp[:].rearrange("p (c i) t -> p c t i", i=4),
-                    in_=u[:, 4 * g : 4 * g + 4, :].rearrange("p t (c i) -> p c t i", i=4),
+                    out=grp[:, 0:n, :].rearrange("p (c i) t -> p c t i", i=4),
+                    in_=u[:, 4 * g : 4 * g + 4, 0:n].rearrange("p t (c i) -> p c t i", i=4),
                 )
                 grps.append(grp)
             for g in range(2):
                 nc.vector.quantize_mx(
-                    out=codes[:, g, :].bitcast(FP8X4),
-                    scales=sc[:, g, :],
-                    in_=grps[g][:].rearrange("p c t -> p (c t)"),
+                    out=codes[:, g, 0:n].bitcast(FP8X4),
+                    scales=sc[:, g, 0:n],
+                    in_=grps[g][:, 0:n, :].rearrange("p c t -> p (c t)"),
                 )
 
         def mx(s):
             if not valid(s):
                 return
+            n = P * WIDTHS[s]
             codes = T["codes", s]
             sc = T["sc", s]
-            for h in range(2):
-                acc = ps_acc.tile([P, SUP], F32, name="acc%d" % h)
+            for h in (1, 0):
+                acc = ps_acc.tile([P, 512], F32, name="acc%d" % h)
                 T["acc%d" % h, s] = acc
                 for g in range(2):
                     nc.tensor.matmul_mx(
-                        out=acc[:],
+                        out=acc[:, 0:n],
                         lhsT=wcodes[:, 2 * h + g, :].bitcast(FP8X4),
                         lhsT_scale=wsc[:, 2 * h + g, :],
-                        rhs=codes[:, g, :].bitcast(FP8X4),
-                        rhs_scale=sc[:, g, :],
+                        rhs=codes[:, g, 0:n].bitcast(FP8X4),
+                        rhs_scale=sc[:, g, 0:n],
                         start=(g == 0),
                         stop=(g == 1),
                     )
@@ -254,24 +302,26 @@ def tile_gau_pb_t_kernel(
         def silu(s):
             if not valid(s):
                 return
-            hgT = epool.tile([P, SUP], F32, name="hgT")
-            nc.scalar.activation(out=hgT[:], in_=T["acc0", s][:], func=ACT.Silu, bias=cols[:, 16:17], scale=1.0)
-            zT = epool.tile([P, SUP], F32, name="zT")
-            nc.scalar.activation(out=zT[:], in_=T["acc1", s][:], func=ACT.Silu, bias=cols[:, 17:18], scale=1.0)
-            T["hg", s] = hgT
-            T["z", s] = zT
-
-        def qk(s):
-            if not valid(s):
-                return
-            zT = T["z", s]
-            for i, nm in enumerate(("q", "k")):
-                t = epool.tile([P, SUP], F32, name=nm + "T")
+            n = P * WIDTHS[s]
+            for nm, acc, c in (("z", "acc1", 17), ("hg", "acc0", 16)):
+                t = epool.tile([P, 512], F32, name=nm + "T")
                 nc.scalar.activation(
-                    out=t[:], in_=zT[:], func=ACT.Identity,
-                    bias=cols[:, 20 + i : 21 + i], scale=cols[:, 18 + i : 19 + i],
+                    out=t[:, 0:n], in_=T[acc, s][:, 0:n], func=ACT.Silu, bias=cols[:, c : c + 1], scale=1.0
                 )
                 T[nm, s] = t
+
+        def qk(s, i):
+            if not valid(s):
+                return
+            n = P * WIDTHS[s]
+            nm = "qk"[i]
+            t = epool.tile([P, 512], F32, name=nm + "T")
+            nc.vector.tensor_scalar(
+                out=t[:, 0:n], in0=T["z", s][:, 0:n],
+                scalar1=cols[:, 18 + i : 19 + i], scalar2=cols[:, 20 + i : 21 + i],
+                op0=ALU.mult, op1=ALU.add,
+            )
+            T[nm, s] = t
 
         def t2(s, nm):
             if not valid(s):
@@ -279,63 +329,71 @@ def tile_gau_pb_t_kernel(
             src = T[nm, s]
             to = ps_out.tile([P, 512], F32, tag="tout", name="to_" + nm)
             T["to_" + nm, s] = to
-            for j in range(JT):
+            for j in range(WIDTHS[s]):
                 nc.tensor.transpose(to[:, P * j : P * (j + 1)], src[:, P * j : P * (j + 1)], ident[:])
 
-        def evac(s, nm, eng="s"):
+        def evac(s, nm):
             if not valid(s):
                 return
+            w = WIDTHS[s]
             to = T["to_" + nm, s]
+            rows = rows_of(s)
             if nm == "hg":
-                dst = opool.tile([P, 2, JT, 64], F32, name="o_hg")
-                o_ap = dst[:]
-                i_ap = to[:].rearrange("p (j h o) -> p h j o", j=JT, h=2)
+                dst = opool.tile([P, 2, 4, 64], F32, name="o_hg")
+                nc.scalar.copy(
+                    out=dst[:, :, 0:w, :], in_=to[:, 0 : P * w].rearrange("p (j h o) -> p h j o", j=w, h=2)
+                )
+                for h, name in enumerate("vg"):
+                    nc.sync.dma_start(
+                        out=outs[name][rows, :].rearrange("(p j) o -> p j o", j=w), in_=dst[:, h, 0:w, :]
+                    )
             else:
-                dst = opool.tile([P, JT, P], F32, name="o_" + nm)
-                o_ap = dst[:].rearrange("p j o -> p (j o)")
-                i_ap = to[:]
-            T["o_" + nm, s] = dst
-            if eng == "s":
-                nc.scalar.copy(out=o_ap, in_=i_ap)
-            else:
-                nc.vector.tensor_copy(out=o_ap, in_=i_ap)
-
-        def store(s, nm):
-            if not valid(s):
-                return
-            rows = slice(SUP * s, SUP * (s + 1))
-            if nm == "hg":
-                o = T["o_hg", s]
-                nc.sync.dma_start(out=outs["v"][rows, :].rearrange("(p j) o -> p j o", j=JT), in_=o[:, 0, :, :])
-                nc.sync.dma_start(out=outs["g"][rows, :].rearrange("(p j) o -> p j o", j=JT), in_=o[:, 1, :, :])
-            else:
-                nc.sync.dma_start(out=outs[nm][rows, :].rearrange("(p j) o -> p j o", j=JT), in_=T["o_" + nm, s][:])
+                dst = opool.tile([P, 512], F32, name="o_" + nm)
+                nc.scalar.copy(out=dst[:, 0 : P * w], in_=to[:, 0 : P * w])
+                nc.sync.dma_start(
+                    out=outs[nm][rows, :].rearrange("(p j) o -> p (j o)", j=w), in_=dst[:, 0 : P * w]
+                )
 
         load(0)
+        load_consts()
         load(1)
+        load_weights()
+        for s in range(2, AHEAD):
+            load(s)
+        for s in range(LEAD):
+            stats(s)
+            last_aggr(s)
+            if s < GATES:
+                gate(s)
         prep_consts()
-        prep_weights()
-        for i in range(NSUP + 5):
-            load(i + 2)
-            stats(i)
+        for i in range(NS + 4):
+            load(i + AHEAD)
+            rstd_stage(i)
+            stats(i + LEAD)
+            if i + LEAD < GATES:
+                last_aggr(i + LEAD)
+                gate(i + LEAD)
+            norm(i, "g")
+            norm(i, "v")
+            mx(i - 2)
+            evac(i - 3, "q")
+            evac(i - 3, "k")
+            silu(i - 2)
+            t2(i - 2, "hg")
+            norm(i, "s")
+            evac(i - 2, "hg")
+            t1c(i)
+            if i == 0:
+                prep_weights()
+            qk(i - 2, 0)
+            if i + LEAD >= GATES:
+                last_aggr(i + LEAD)
+            qk(i - 2, 1)
+            t2(i - 2, "q")
+            t2(i - 2, "k")
+            regroup_quant(i - 1)
             if i == 1:
                 quant_weights()
-            nmr_stage(i - 1)
-            norm(i - 1, "g")
-            rstd_stage(i)
-            norm(i - 1, "s")
-            mx(i - 3)
-            t2(i - 4, "q")
-            t2(i - 4, "k")
-            silu(i - 3)
-            t2(i - 3, "hg")
-            evac(i - 4, "q")
-            evac(i - 4, "k")
-            store(i - 4, "q")
-            store(i - 4, "k")
-            evac(i - 3, "hg")
-            store(i - 3, "hg")
-            t1c(i - 1)
-            qk(i - 3)
-            regroup_quant(i - 2)
-            gate(i)
+            if i + 1 >= GATES:
+                gate(i + 1)
+            evac_v(i)

@@ -18,12 +18,11 @@ KB = D // P
 EPS = 1e-5
 FLOPS = 2 * ROWS * D * 256
 
-WIDTHS = [1, 1, 2] + [4] * 14 + [2, 1, 1]
+WIDTHS = [2] + [4] * 15 + [2]
 FIRST = [sum(WIDTHS[:s]) for s in range(len(WIDTHS))]
 NS = len(WIDTHS)
 AHEAD = 4
-LEAD = 1
-GATES = 3
+FILL = (0, 0, 0, 0)
 
 
 def owners(s):
@@ -33,8 +32,12 @@ def owners(s):
     return {1: "s", 2: "gs", 4: "gggs"}[w]
 
 
-def vshare(s):
-    return 3 if s >= NS - 4 else 0
+def vector_blocks(s):
+    return ()
+
+
+def vector_outputs(s):
+    return ""
 
 
 def tile_gau_pb_t_kernel(
@@ -62,7 +65,8 @@ def tile_gau_pb_t_kernel(
         opool = ctx.enter_context(tc.tile_pool(name="opool", bufs=2))
         ps_in = ctx.enter_context(tc.psum_pool(name="ps_in", bufs=3))
         ps_acc = ctx.enter_context(tc.psum_pool(name="ps_acc", bufs=1))
-        ps_out = ctx.enter_context(tc.psum_pool(name="ps_out", bufs=3))
+        ps_out = ctx.enter_context(tc.psum_pool(name="ps_out", bufs=2))
+        ps_warm = ctx.enter_context(tc.psum_pool(name="ps_warm", bufs=1))
 
         T = {}
 
@@ -76,6 +80,10 @@ def tile_gau_pb_t_kernel(
         cst_p = keep.tile([P, 640], BF16, name="cst_p")
         mhalf = keep.tile([P, 4], F32, name="mhalf")
         nc.vector.memset(mhalf[:], -0.5)
+        sts = [keep.tile([P, 4, 15], F32, name="st%d" % s) for s in range(4)]
+        for st in sts:
+            nc.vector.memset(st[:], 0.0)
+            nc.vector.memset(st[:, :, 14:15], EPS * D)
         nc.scalar.activation(out=warm[:], in_=warm[:], func=ACT.Silu)
         ident = keep.tile([P, P], F32, name="ident")
         make_identity(nc, ident[:])
@@ -154,35 +162,26 @@ def tile_gau_pb_t_kernel(
                 return
             w = WIDTHS[s]
             xs = T["xs", s]
-            st = small.tile([P, 4, 2, 6], F32, name="st")
             mv = small.tile([P, 4, 2], F32, name="mv")
-            T["st", s] = st
             T["mv", s] = mv
             for j in range(w):
                 for c in range(2):
-                    nc.vector.bn_stats(out=st[:, j, c, :], in_=xs[:, j, 512 * c : 512 * (c + 1)])
+                    nc.vector.bn_stats(
+                        out=sts[s % 4][:, j, 6 * c : 6 * (c + 1)], in_=xs[:, j, 512 * c : 512 * (c + 1)]
+                    )
                 if j > 0:
                     aggr(s, j - 1)
 
         def aggr(s, j):
-            nc.vector.bn_aggr(
-                out=T["mv", s][:, j, :], in_=T["st", s][:, j, :, :].rearrange("p c v -> p (c v)")
-            )
-
-        def last_aggr(s):
-            if valid(s):
-                aggr(s, WIDTHS[s] - 1)
+            nc.vector.bn_aggr(out=T["mv", s][:, j, :], in_=sts[s % 4][:, j, :])
 
         def gate(s):
             if not valid(s):
                 return
             w = WIDTHS[s]
-            mv = T["mv", s]
-            ve = small.tile([P, 4], F32, name="ve")
-            nc.vector.tensor_scalar_add(out=ve[:, 0:w], in0=mv[:, 0:w, 1], scalar1=EPS)
+            aggr(s, w - 1)
             negmu = small.tile([P, 4], F32, name="negmu")
-            nc.vector.tensor_scalar_mul(out=negmu[:, 0:w], in0=mv[:, 0:w, 0], scalar1=-1.0)
-            T["ve", s] = ve
+            nc.vector.tensor_scalar_mul(out=negmu[:, 0:w], in0=T["mv", s][:, 0:w, 0], scalar1=-1.0)
             T["negmu", s] = negmu
 
         def rstd_stage(s):
@@ -190,7 +189,7 @@ def tile_gau_pb_t_kernel(
                 return
             w = WIDTHS[s]
             rstd = small.tile([P, 4], F32, name="rstd")
-            nc.gpsimd.tensor_tensor(out=rstd[:, 0:w], in0=T["ve", s][:, 0:w], in1=mhalf[:, 0:w], op=ALU.pow)
+            nc.gpsimd.tensor_tensor(out=rstd[:, 0:w], in0=T["mv", s][:, 0:w, 1], in1=mhalf[:, 0:w], op=ALU.pow)
             T["rstd", s] = rstd
             if "s" in owners(s):
                 nmr = small.tile([P, 4], F32, name="nmr")
@@ -225,90 +224,100 @@ def tile_gau_pb_t_kernel(
                         op0=ALU.add, op1=ALU.mult,
                     )
 
-        def t1c(s):
+        busy = ps_warm.tile([P, 512], F32, name="busy")
+
+        def t1(s, kbs):
             if not valid(s):
                 return
             w = WIDTHS[s]
             n = P * w
             y = T["y", s]
-            u = upool.tile([P, KB, 512], BF16, name="u")
-            T["u", s] = u
-            for kb in range(KB):
+            if ("u", s) not in T:
+                T["u", s] = upool.tile([P, KB, 512], BF16, name="u")
+            u = T["u", s]
+            for kb in kbs:
                 tp = ps_in.tile([P, 512], F32, tag="tin", name="tp")
-                T["tp%d" % kb, s] = tp
                 c0 = 256 * (kb % 4) + P * (kb // 4)
                 for j in range(w):
                     nc.tensor.transpose(tp[:, P * j : P * (j + 1)], y[:, j, c0 : c0 + P], ident[:])
-                if kb < KB - vshare(s):
+                if kb in vector_blocks(s):
+                    nc.vector.tensor_scalar(
+                        out=u[:, kb, 0:n], in0=tp[:, 0:n], scalar1=cols[:, kb : kb + 1],
+                        scalar2=cols[:, 8 + kb : 9 + kb], op0=ALU.mult, op1=ALU.add,
+                    )
+                else:
                     nc.scalar.activation(
                         out=u[:, kb, 0:n], in_=tp[:, 0:n], func=ACT.Identity,
                         bias=cols[:, 8 + kb : 9 + kb], scale=cols[:, kb : kb + 1],
                     )
 
-        def evac_v(s):
+        def regroup(s):
             if not valid(s):
                 return
             n = P * WIDTHS[s]
-            for kb in range(KB - vshare(s), KB):
-                nc.vector.tensor_scalar(
-                    out=T["u", s][:, kb, 0:n], in0=T["tp%d" % kb, s][:, 0:n],
-                    scalar1=cols[:, kb : kb + 1], scalar2=cols[:, 8 + kb : 9 + kb], op0=ALU.mult, op1=ALU.add,
-                )
+            grp = gpool.tile([P, 4096], BF16, name="grp", align_bytes=64)
+            T["grp", s] = grp
+            nc.vector.tensor_copy(
+                out=grp[:, 0 : 8 * n].rearrange("p (g c i t) -> p g c t i", g=2, i=4, t=4),
+                in_=T["u", s][:, :, 0:n].rearrange("p (g t) (c i) -> p g c t i", g=2, i=4),
+            )
 
-        def regroup_quant(s):
+        def quant(s):
             if not valid(s):
                 return
             n = P * WIDTHS[s]
-            u = T["u", s]
-            codes = cpool.tile([P, 2, 512], U32, name="codes", align_bytes=64)
-            sc = cpool.tile([P, 2, 512], U8, name="sc", align_bytes=64)
-            T["codes", s] = codes
-            T["sc", s] = sc
-            grps = []
-            for g in range(2):
-                grp = gpool.tile([P, 512, 4], BF16, name="grp%d" % g, align_bytes=64)
-                nc.vector.tensor_copy(
-                    out=grp[:, 0:n, :].rearrange("p (c i) t -> p c t i", i=4),
-                    in_=u[:, 4 * g : 4 * g + 4, 0:n].rearrange("p t (c i) -> p c t i", i=4),
-                )
-                grps.append(grp)
-            for g in range(2):
-                nc.vector.quantize_mx(
-                    out=codes[:, g, 0:n].bitcast(FP8X4),
-                    scales=sc[:, g, 0:n],
-                    in_=grps[g][:, 0:n, :].rearrange("p c t -> p (c t)"),
-                )
+            codes = cpool.tile([P, 1024], U32, name="codes", align_bytes=64)
+            sc = cpool.tile([P, 1024], U8, name="sc", align_bytes=64)
+            T["codes", s] = [codes[:, n * g : n * (g + 1)].bitcast(FP8X4) for g in range(2)]
+            T["sc", s] = [sc[:, n * g : n * (g + 1)] for g in range(2)]
+            nc.vector.quantize_mx(
+                out=codes[:, 0 : 2 * n].bitcast(FP8X4), scales=sc[:, 0 : 2 * n], in_=T["grp", s][:, 0 : 8 * n]
+            )
 
-        def mx(s):
+        def mx(s, h):
             if not valid(s):
                 return
             n = P * WIDTHS[s]
             codes = T["codes", s]
             sc = T["sc", s]
-            for h in (1, 0):
-                acc = ps_acc.tile([P, 512], F32, name="acc%d" % h)
-                T["acc%d" % h, s] = acc
-                for g in range(2):
-                    nc.tensor.matmul_mx(
-                        out=acc[:, 0:n],
-                        lhsT=wcodes[:, 2 * h + g, :].bitcast(FP8X4),
-                        lhsT_scale=wsc[:, 2 * h + g, :],
-                        rhs=codes[:, g, 0:n].bitcast(FP8X4),
-                        rhs_scale=sc[:, g, 0:n],
-                        start=(g == 0),
-                        stop=(g == 1),
-                    )
+            acc = ps_acc.tile([P, 512], F32, name="acc%d" % h)
+            T["acc%d" % h, s] = acc
+            for g in range(2):
+                nc.tensor.matmul_mx(
+                    out=acc[:, 0:n],
+                    lhsT=wcodes[:, 2 * h + g, :].bitcast(FP8X4),
+                    lhsT_scale=wsc[:, 2 * h + g, :],
+                    rhs=codes[g],
+                    rhs_scale=sc[g],
+                    start=(g == 0),
+                    stop=(g == 1),
+                )
 
-        def silu(s):
+        def keep_busy(s, count):
+            if not valid(s) or WIDTHS[s] < 4:
+                return
+            for d in range(count):
+                g = d % 2
+                nc.tensor.matmul_mx(
+                    out=busy[:],
+                    lhsT=wcodes[:, g, :].bitcast(FP8X4),
+                    lhsT_scale=wsc[:, g, :],
+                    rhs=T["codes", s][g],
+                    rhs_scale=T["sc", s][g],
+                    start=True,
+                    stop=True,
+                )
+
+        def silu(s, h):
             if not valid(s):
                 return
             n = P * WIDTHS[s]
-            for nm, acc, c in (("z", "acc1", 17), ("hg", "acc0", 16)):
-                t = epool.tile([P, 512], F32, name=nm + "T")
-                nc.scalar.activation(
-                    out=t[:, 0:n], in_=T[acc, s][:, 0:n], func=ACT.Silu, bias=cols[:, c : c + 1], scale=1.0
-                )
-                T[nm, s] = t
+            nm = ("hg", "z")[h]
+            t = epool.tile([P, 512], F32, name=nm + "T")
+            nc.scalar.activation(
+                out=t[:, 0:n], in_=T["acc%d" % h, s][:, 0:n], func=ACT.Silu, bias=cols[:, 16 + h : 17 + h], scale=1.0
+            )
+            T[nm, s] = t
 
         def qk(s, i):
             if not valid(s):
@@ -335,12 +344,13 @@ def tile_gau_pb_t_kernel(
         def evac(s, nm):
             if not valid(s):
                 return
+            copy = nc.vector.tensor_copy if nm in vector_outputs(s) else nc.scalar.copy
             w = WIDTHS[s]
             to = T["to_" + nm, s]
             rows = rows_of(s)
             if nm == "hg":
                 dst = opool.tile([P, 2, 4, 64], F32, name="o_hg")
-                nc.scalar.copy(
+                copy(
                     out=dst[:, :, 0:w, :], in_=to[:, 0 : P * w].rearrange("p (j h o) -> p h j o", j=w, h=2)
                 )
                 for h, name in enumerate("vg"):
@@ -349,7 +359,7 @@ def tile_gau_pb_t_kernel(
                     )
             else:
                 dst = opool.tile([P, 512], F32, name="o_" + nm)
-                nc.scalar.copy(out=dst[:, 0 : P * w], in_=to[:, 0 : P * w])
+                copy(out=dst[:, 0 : P * w], in_=to[:, 0 : P * w])
                 nc.sync.dma_start(
                     out=outs[nm][rows, :].rearrange("(p j) o -> p (j o)", j=w), in_=dst[:, 0 : P * w]
                 )
@@ -360,40 +370,38 @@ def tile_gau_pb_t_kernel(
         load_weights()
         for s in range(2, AHEAD):
             load(s)
-        for s in range(LEAD):
-            stats(s)
-            last_aggr(s)
-            if s < GATES:
-                gate(s)
+        stats(0)
         prep_consts()
-        for i in range(NS + 4):
+        prep_weights()
+        for i in range(-1, NS + 3):
             load(i + AHEAD)
-            rstd_stage(i)
-            stats(i + LEAD)
-            if i + LEAD < GATES:
-                last_aggr(i + LEAD)
-                gate(i + LEAD)
-            norm(i, "g")
-            norm(i, "v")
-            mx(i - 2)
-            evac(i - 3, "q")
-            evac(i - 3, "k")
-            silu(i - 2)
-            t2(i - 2, "hg")
-            norm(i, "s")
-            evac(i - 2, "hg")
-            t1c(i)
-            if i == 0:
-                prep_weights()
+            regroup(i - 1)
             qk(i - 2, 0)
-            if i + LEAD >= GATES:
-                last_aggr(i + LEAD)
             qk(i - 2, 1)
+            quant(i - 1)
+            t1(i, (0, 1))
+            t2(i - 2, "hg")
+            evac(i - 2, "hg")
+            keep_busy(i - 2, FILL[0])
+            t1(i, (2, 3))
             t2(i - 2, "q")
+            evac(i - 2, "q")
+            keep_busy(i - 2, FILL[1])
+            t1(i, (4, 5))
             t2(i - 2, "k")
-            regroup_quant(i - 1)
-            if i == 1:
+            evac(i - 2, "k")
+            mx(i - 1, 1)
+            keep_busy(i - 1, FILL[2])
+            silu(i - 1, 1)
+            t1(i, (6, 7))
+            gate(i + 1)
+            rstd_stage(i + 1)
+            stats(i + 2)
+            norm(i + 1, "g")
+            norm(i + 1, "v")
+            norm(i + 1, "s")
+            mx(i - 1, 0)
+            keep_busy(i - 1, FILL[3])
+            silu(i - 1, 0)
+            if i == 0:
                 quant_weights()
-            if i + 1 >= GATES:
-                gate(i + 1)
-            evac_v(i)

@@ -22,7 +22,8 @@ WIDTHS = [2] + [4] * 15 + [2]
 FIRST = [sum(WIDTHS[:s]) for s in range(len(WIDTHS))]
 NS = len(WIDTHS)
 AHEAD = 4
-FILL = (0, 0, 0, 0)
+NL = 1
+COUNTED = ()
 
 
 def owners(s):
@@ -38,6 +39,10 @@ def vector_blocks(s):
 
 def vector_outputs(s):
     return ""
+
+
+def qk_engine(s):
+    return "vs"
 
 
 def tile_gau_pb_t_kernel(
@@ -57,7 +62,7 @@ def tile_gau_pb_t_kernel(
         keep = ctx.enter_context(tc.tile_pool(name="keep", bufs=1))
         xpool = ctx.enter_context(tc.tile_pool(name="xpool", bufs=7))
         small = ctx.enter_context(tc.tile_pool(name="small", bufs=4))
-        ypool = ctx.enter_context(tc.tile_pool(name="ypool", bufs=2))
+        ypool = ctx.enter_context(tc.tile_pool(name="ypool", bufs=3))
         upool = ctx.enter_context(tc.tile_pool(name="upool", bufs=2))
         gpool = ctx.enter_context(tc.tile_pool(name="gpool", bufs=2))
         cpool = ctx.enter_context(tc.tile_pool(name="cpool", bufs=2))
@@ -65,8 +70,7 @@ def tile_gau_pb_t_kernel(
         opool = ctx.enter_context(tc.tile_pool(name="opool", bufs=2))
         ps_in = ctx.enter_context(tc.psum_pool(name="ps_in", bufs=3))
         ps_acc = ctx.enter_context(tc.psum_pool(name="ps_acc", bufs=1))
-        ps_out = ctx.enter_context(tc.psum_pool(name="ps_out", bufs=2))
-        ps_warm = ctx.enter_context(tc.psum_pool(name="ps_warm", bufs=1))
+        ps_out = ctx.enter_context(tc.psum_pool(name="ps_out", bufs=3))
 
         T = {}
 
@@ -175,11 +179,14 @@ def tile_gau_pb_t_kernel(
         def aggr(s, j):
             nc.vector.bn_aggr(out=T["mv", s][:, j, :], in_=sts[s % 4][:, j, :])
 
+        def agl(s):
+            if valid(s):
+                aggr(s, WIDTHS[s] - 1)
+
         def gate(s):
             if not valid(s):
                 return
             w = WIDTHS[s]
-            aggr(s, w - 1)
             negmu = small.tile([P, 4], F32, name="negmu")
             nc.vector.tensor_scalar_mul(out=negmu[:, 0:w], in0=T["mv", s][:, 0:w, 0], scalar1=-1.0)
             T["negmu", s] = negmu
@@ -191,12 +198,16 @@ def tile_gau_pb_t_kernel(
             rstd = small.tile([P, 4], F32, name="rstd")
             nc.gpsimd.tensor_tensor(out=rstd[:, 0:w], in0=T["mv", s][:, 0:w, 1], in1=mhalf[:, 0:w], op=ALU.pow)
             T["rstd", s] = rstd
-            if "s" in owners(s):
-                nmr = small.tile([P, 4], F32, name="nmr")
-                nc.gpsimd.tensor_tensor(
-                    out=nmr[:, 0:w], in0=T["negmu", s][:, 0:w], in1=rstd[:, 0:w], op=ALU.mult
-                )
-                T["nmr", s] = nmr
+
+        def nmr_stage(s):
+            if not valid(s) or "s" not in owners(s):
+                return
+            w = WIDTHS[s]
+            nmr = small.tile([P, 4], F32, name="nmr")
+            nc.gpsimd.tensor_tensor(
+                out=nmr[:, 0:w], in0=T["negmu", s][:, 0:w], in1=T["rstd", s][:, 0:w], op=ALU.mult
+            )
+            T["nmr", s] = nmr
 
         def norm(s, eng):
             if not valid(s):
@@ -223,8 +234,6 @@ def tile_gau_pb_t_kernel(
                         scalar1=T["negmu", s][:, j : j + 1], scalar2=rstd[:, j : j + 1],
                         op0=ALU.add, op1=ALU.mult,
                     )
-
-        busy = ps_warm.tile([P, 512], F32, name="busy")
 
         def t1(s, kbs):
             if not valid(s):
@@ -293,21 +302,6 @@ def tile_gau_pb_t_kernel(
                     stop=(g == 1),
                 )
 
-        def keep_busy(s, count):
-            if not valid(s) or WIDTHS[s] < 4:
-                return
-            for d in range(count):
-                g = d % 2
-                nc.tensor.matmul_mx(
-                    out=busy[:],
-                    lhsT=wcodes[:, g, :].bitcast(FP8X4),
-                    lhsT_scale=wsc[:, g, :],
-                    rhs=T["codes", s][g],
-                    rhs_scale=T["sc", s][g],
-                    start=True,
-                    stop=True,
-                )
-
         def silu(s, h):
             if not valid(s):
                 return
@@ -319,17 +313,20 @@ def tile_gau_pb_t_kernel(
             )
             T[nm, s] = t
 
-        def qk(s, i):
-            if not valid(s):
+        def qk(s, i, eng):
+            if not valid(s) or qk_engine(s)[i] != eng:
                 return
             n = P * WIDTHS[s]
             nm = "qk"[i]
             t = epool.tile([P, 512], F32, name=nm + "T")
-            nc.vector.tensor_scalar(
-                out=t[:, 0:n], in0=T["z", s][:, 0:n],
-                scalar1=cols[:, 18 + i : 19 + i], scalar2=cols[:, 20 + i : 21 + i],
-                op0=ALU.mult, op1=ALU.add,
-            )
+            gam = cols[:, 18 + i : 19 + i]
+            bet = cols[:, 20 + i : 21 + i]
+            if eng == "v":
+                nc.vector.tensor_scalar(
+                    out=t[:, 0:n], in0=T["z", s][:, 0:n], scalar1=gam, scalar2=bet, op0=ALU.mult, op1=ALU.add
+                )
+            else:
+                nc.scalar.activation(out=t[:, 0:n], in_=T["z", s][:, 0:n], func=ACT.Identity, bias=bet, scale=gam)
             T[nm, s] = t
 
         def t2(s, nm):
@@ -339,7 +336,11 @@ def tile_gau_pb_t_kernel(
             to = ps_out.tile([P, 512], F32, tag="tout", name="to_" + nm)
             T["to_" + nm, s] = to
             for j in range(WIDTHS[s]):
-                nc.tensor.transpose(to[:, P * j : P * (j + 1)], src[:, P * j : P * (j + 1)], ident[:])
+                piece = src[:, P * j : P * (j + 1)]
+                if nm in COUNTED:
+                    nc.tensor.matmul(to[:, P * j : P * (j + 1)], lhsT=piece, rhs=ident[:], start=True, stop=True)
+                else:
+                    nc.tensor.transpose(to[:, P * j : P * (j + 1)], piece, ident[:])
 
         def evac(s, nm):
             if not valid(s):
@@ -373,35 +374,36 @@ def tile_gau_pb_t_kernel(
         stats(0)
         prep_consts()
         prep_weights()
-        for i in range(-1, NS + 3):
-            load(i + AHEAD)
-            regroup(i - 1)
-            qk(i - 2, 0)
-            qk(i - 2, 1)
-            quant(i - 1)
-            t1(i, (0, 1))
-            t2(i - 2, "hg")
-            evac(i - 2, "hg")
-            keep_busy(i - 2, FILL[0])
-            t1(i, (2, 3))
-            t2(i - 2, "q")
-            evac(i - 2, "q")
-            keep_busy(i - 2, FILL[1])
-            t1(i, (4, 5))
-            t2(i - 2, "k")
-            evac(i - 2, "k")
-            mx(i - 1, 1)
-            keep_busy(i - 1, FILL[2])
-            silu(i - 1, 1)
-            t1(i, (6, 7))
-            gate(i + 1)
-            rstd_stage(i + 1)
-            stats(i + 2)
-            norm(i + 1, "g")
-            norm(i + 1, "v")
-            norm(i + 1, "s")
-            mx(i - 1, 0)
-            keep_busy(i - 1, FILL[3])
-            silu(i - 1, 0)
+        for i in range(-NL, NS + 3):
+            if i + AHEAD >= AHEAD:
+                load(i + AHEAD)
+            qk(i-2,0,"v")
+            agl(i+1)
+            rstd_stage(i+1)
+            qk(i-2,1,"v")
+            regroup(i-1)
+            quant(i-1)
+            t1(i,(0,1))
+            t2(i-2,"hg")
+            evac(i-3,"k")
+            t1(i,(2,3))
+            t2(i-2,"q")
+            evac(i-2,"hg")
+            t1(i,(4,5))
+            t2(i-2,"k")
+            evac(i-2,"q")
+            gate(i+1)
+            nmr_stage(i+1)
+            stats(i+2)
+            norm(i+1,"g")
+            norm(i+1,"v")
+            norm(i+1,"s")
+            t1(i,(6,7))
+            mx(i-1,1)
+            mx(i-1,0)
+            silu(i-1,1)
+            qk(i-1,0,"s")
+            qk(i-1,1,"s")
+            silu(i-1,0)
             if i == 0:
                 quant_weights()

@@ -23,6 +23,13 @@ FIRST = [sum(WIDTHS[:s]) for s in range(len(WIDTHS))]
 NS = len(WIDTHS)
 AHEAD = 4
 NL = 1
+EARLY = ()
+G_T = 1
+NMR = "s"
+RG_S = 0
+QK_S = 0
+QK_V = 3
+QW = 0
 COUNTED = ()
 
 
@@ -42,7 +49,7 @@ def vector_outputs(s):
 
 
 def qk_engine(s):
-    return "vs"
+    return "ss" if s < QK_S else "vv" if s >= NS - QK_V else "vs"
 
 
 def tile_gau_pb_t_kernel(
@@ -159,7 +166,12 @@ def tile_gau_pb_t_kernel(
             w = WIDTHS[s]
             xs = xpool.tile([P, 4, D], BF16, name="xs")
             T["xs", s] = xs
-            nc.sync.dma_start(out=xs[:, 0:w, :], in_=xf[rows_of(s), :].rearrange("(p j) k -> p j k", j=w))
+            src = xf[rows_of(s), :].rearrange("(p j) k -> p j k", j=w)
+            if s == 0:
+                for j in range(w):
+                    nc.sync.dma_start(out=xs[:, j, :], in_=src[:, j, :])
+            else:
+                nc.sync.dma_start(out=xs[:, 0:w, :], in_=src)
 
         def stats(s):
             if not valid(s):
@@ -183,6 +195,13 @@ def tile_gau_pb_t_kernel(
             if valid(s):
                 aggr(s, WIDTHS[s] - 1)
 
+        def early(s):
+            if s in EARLY:
+                agl(s)
+                rstd_stage(s)
+                gate(s)
+                nmr_stage(s)
+
         def gate(s):
             if not valid(s):
                 return
@@ -200,13 +219,25 @@ def tile_gau_pb_t_kernel(
             T["rstd", s] = rstd
 
         def nmr_stage(s):
-            if not valid(s) or "s" not in owners(s):
+            if not valid(s) or not ("s" in owners(s) or "h" in owners(s)):
                 return
             w = WIDTHS[s]
             nmr = small.tile([P, 4], F32, name="nmr")
-            nc.gpsimd.tensor_tensor(
-                out=nmr[:, 0:w], in0=T["negmu", s][:, 0:w], in1=T["rstd", s][:, 0:w], op=ALU.mult
-            )
+            if NMR == "s":
+                for j in range(w):
+                    if owners(s)[j] in "sh":
+                        nc.scalar.activation(
+                            out=nmr[:, j : j + 1], in_=T["negmu", s][:, j : j + 1], func=ACT.Copy,
+                            scale=T["rstd", s][:, j : j + 1],
+                        )
+            elif NMR == "v":
+                nc.vector.tensor_tensor(
+                    out=nmr[:, 0:w], in0=T["negmu", s][:, 0:w], in1=T["rstd", s][:, 0:w], op=ALU.mult
+                )
+            else:
+                nc.gpsimd.tensor_tensor(
+                    out=nmr[:, 0:w], in0=T["negmu", s][:, 0:w], in1=T["rstd", s][:, 0:w], op=ALU.mult
+                )
             T["nmr", s] = nmr
 
         def norm(s, eng):
@@ -218,10 +249,16 @@ def tile_gau_pb_t_kernel(
             xs = T["xs", s]
             rstd = T["rstd", s]
             for j in range(WIDTHS[s]):
-                if owners(s)[j] != eng:
+                who = owners(s)[j]
+                t0, t1_ = 0, 4
+                if who == "h":
+                    t0, t1_ = (0, G_T) if eng == "g" else (G_T, 4)
+                    if eng == "v":
+                        continue
+                elif who != eng:
                     continue
-                y_j = y[:, j, :].rearrange("p (t m r) -> p t m r", t=4, r=8)
-                x_j = xs[:, j, :].rearrange("p (m t r) -> p t m r", t=4, r=8)
+                y_j = y[:, j, 256 * t0 : 256 * t1_].rearrange("p (t m r) -> p t m r", t=t1_ - t0, r=8)
+                x_j = xs[:, j, :].rearrange("p (m t r) -> p t m r", t=4, r=8)[:, t0:t1_, :, :]
                 if eng == "s":
                     nc.scalar.activation(
                         out=y_j, in_=x_j, func=ACT.Identity,
@@ -229,6 +266,9 @@ def tile_gau_pb_t_kernel(
                     )
                 else:
                     e = nc.gpsimd if eng == "g" else nc.vector
+                    if eng == "g":
+                        y_j = y[:, j, :].rearrange("p (t m r) -> p m t r", t=4, r=8)
+                        x_j = xs[:, j, :].rearrange("p (m t r) -> p m t r", t=4, r=8)
                     e.tensor_scalar(
                         out=y_j, in0=x_j,
                         scalar1=T["negmu", s][:, j : j + 1], scalar2=rstd[:, j : j + 1],
@@ -266,7 +306,8 @@ def tile_gau_pb_t_kernel(
             n = P * WIDTHS[s]
             grp = gpool.tile([P, 4096], BF16, name="grp", align_bytes=64)
             T["grp", s] = grp
-            nc.vector.tensor_copy(
+            copy = nc.scalar.copy if s < RG_S else nc.vector.tensor_copy
+            copy(
                 out=grp[:, 0 : 8 * n].rearrange("p (g c i t) -> p g c t i", g=2, i=4, t=4),
                 in_=T["u", s][:, :, 0:n].rearrange("p (g t) (c i) -> p g c t i", g=2, i=4),
             )
@@ -389,11 +430,13 @@ def tile_gau_pb_t_kernel(
             t1(i,(2,3))
             t2(i-2,"q")
             evac(i-2,"hg")
+            gate(i+1)
             t1(i,(4,5))
             t2(i-2,"k")
-            evac(i-2,"q")
-            gate(i+1)
             nmr_stage(i+1)
+            evac(i-2,"q")
+            if i == 0:
+                quant_weights()
             stats(i+2)
             norm(i+1,"g")
             norm(i+1,"v")
@@ -405,5 +448,3 @@ def tile_gau_pb_t_kernel(
             qk(i-1,0,"s")
             qk(i-1,1,"s")
             silu(i-1,0)
-            if i == 0:
-                quant_weights()

from contextlib import ExitStack

import concourse.mybir as mybir
from concourse.masks import make_identity

F32 = mybir.dt.float32
BF16 = mybir.dt.bfloat16
U32 = mybir.dt.uint32
U8 = mybir.dt.uint8
FP8X4 = mybir.dt.float8_e4m3fn_x4
ALU = mybir.AluOpType
ACT = mybir.ActivationFunctionType

P = 128
D = 1024
ROWS = 8192
KB = D // P
EPS = 1e-5
FLOPS = 2 * ROWS * D * 256

WIDTHS = [2] + [4] * 15 + [2]
FIRST = [sum(WIDTHS[:s]) for s in range(len(WIDTHS))]
NS = len(WIDTHS)
AHEAD = 4
NL = 1
EARLY = ()
G_T = 1
NMR = "s"
RG_S = 0
QK_S = 0
QK_V = 3
QW = 0
COUNTED = ()


def owners(s):
    w = WIDTHS[s]
    if s >= NS - 2:
        return "v" * w
    return {1: "s", 2: "gs", 4: "gggs"}[w]


def vector_blocks(s):
    return ()


def vector_outputs(s):
    return ""


def qk_engine(s):
    return "ss" if s < QK_S else "vv" if s >= NS - QK_V else "vs"


def tile_gau_pb_t_kernel(
    tc, x, ln_w, ln_b, W_hidden, b_hidden, W_qk, b_qk, gamma, beta, out_0, out_1, out_2, out_3
):
    nc = tc.nc
    xf = x.flatten_outer_dims()
    outs = {
        "v": out_0.flatten_outer_dims(),
        "g": out_1.flatten_outer_dims(),
        "q": out_2.flatten_outer_dims(),
        "k": out_3.flatten_outer_dims(),
    }

    with ExitStack() as ctx:
        ctx.enter_context(tc.manual_schedule())
        keep = ctx.enter_context(tc.tile_pool(name="keep", bufs=1))
        xpool = ctx.enter_context(tc.tile_pool(name="xpool", bufs=7))
        small = ctx.enter_context(tc.tile_pool(name="small", bufs=4))
        ypool = ctx.enter_context(tc.tile_pool(name="ypool", bufs=3))
        upool = ctx.enter_context(tc.tile_pool(name="upool", bufs=2))
        gpool = ctx.enter_context(tc.tile_pool(name="gpool", bufs=2))
        cpool = ctx.enter_context(tc.tile_pool(name="cpool", bufs=2))
        epool = ctx.enter_context(tc.tile_pool(name="epool", bufs=2))
        opool = ctx.enter_context(tc.tile_pool(name="opool", bufs=2))
        ps_in = ctx.enter_context(tc.psum_pool(name="ps_in", bufs=3))
        ps_acc = ctx.enter_context(tc.psum_pool(name="ps_acc", bufs=1))
        ps_out = ctx.enter_context(tc.psum_pool(name="ps_out", bufs=3))

        T = {}

        def valid(s):
            return 0 <= s < NS

        warm = keep.tile([P, 1], F32, name="warm")
        nc.vector.memset(warm[:], 0.0)
        cst_b = keep.tile([P, 640], BF16, name="cst_b")
        nc.vector.memset(cst_b[:], 0.0)
        cst_p = keep.tile([P, 640], BF16, name="cst_p")
        mhalf = keep.tile([P, 4], F32, name="mhalf")
        nc.vector.memset(mhalf[:], -0.5)
        sts = [keep.tile([P, 4, 15], F32, name="st%d" % s) for s in range(4)]
        for st in sts:
            nc.vector.memset(st[:], 0.0)
            nc.vector.memset(st[:, :, 14:15], EPS * D)
        nc.scalar.activation(out=warm[:], in_=warm[:], func=ACT.Silu)
        ident = keep.tile([P, P], F32, name="ident")
        make_identity(nc, ident[:])
        ident_b = keep.tile([P, P], BF16, name="ident_b")
        make_identity(nc, ident_b[:])
        cols = keep.tile([P, 32], F32, name="cols")
        wbs = [keep.tile([P, D], BF16, name="wb%d" % h) for h in range(2)]
        wps = [keep.tile([P, D], BF16, name="wp%d" % h) for h in range(2)]
        wgrp = keep.tile([P, 4, P, 4], BF16, name="wgrp", align_bytes=64)
        wcodes = keep.tile([P, 4, P], U32, name="wcodes", align_bytes=64)
        wsc = keep.tile([P, 4, P], U8, name="wsc", align_bytes=64)

        def load_consts():
            for r0, vec in ((0, ln_w), (2, ln_b)):
                nc.sync.dma_start(out=cst_b[r0 : r0 + 2, 0:512], in_=vec.rearrange("(g f) -> g f", f=512))
            nc.sync.dma_start(out=cst_b[0:1, 512:640], in_=b_hidden.rearrange("(a b) -> a b", b=P))
            nc.sync.dma_start(out=cst_b[1:2, 512:640], in_=b_qk.rearrange("(a b) -> a b", b=P))
            nc.sync.dma_start(out=cst_b[2:4, 512:640], in_=gamma)
            nc.sync.dma_start(out=cst_b[4:6, 512:640], in_=beta)

        def load_weights():
            for h, W in enumerate((W_hidden, W_qk)):
                nc.sync.dma_start(out=wbs[h][:], in_=W)

        def prep_consts():
            nc.scalar.copy(
                out=cst_p[:, 0:512].rearrange("p (t m r) -> p t m r", t=4, r=8),
                in_=cst_b[:, 0:512].rearrange("p (m t r) -> p t m r", t=4, r=8),
            )
            tpc = ps_in.tile([P, 1024], BF16, tag="tin", name="tpc")
            for t in range(4):
                nc.tensor.transpose(tpc[:, P * t : P * (t + 1)], cst_p[:, P * t : P * (t + 1)], ident_b[:])
            nc.tensor.transpose(tpc[:, 512:640], cst_b[:, 512:640], ident_b[:])
            nc.scalar.copy(
                out=cols[:, 0:16].rearrange("p (v t) -> p v t", t=4),
                in_=tpc[:, 0:512].rearrange("p (t c) -> p c t", t=4)[:, 0:4, :],
            )
            nc.scalar.copy(out=cols[:, 16:22], in_=tpc[:, 512:518])

        def prep_weights():
            for h in range(2):
                nc.scalar.copy(
                    out=wps[h][:].rearrange("p (t m r) -> p t m r", t=4, r=8),
                    in_=wbs[h][:].rearrange("p (m t r) -> p t m r", t=4, r=8),
                )
            for h in range(2):
                for g in range(2):
                    tpw = ps_in.tile([P, 1024], BF16, tag="tin", name="tpw")
                    for t in range(4):
                        c0 = 256 * t + P * g
                        nc.tensor.transpose(tpw[:, P * t : P * (t + 1)], wps[h][:, c0 : c0 + P], ident_b[:])
                    nc.scalar.copy(
                        out=wgrp[:, 2 * h + g, :, :], in_=tpw[:, 0:512].rearrange("p (t o) -> p o t", t=4)
                    )

        def quant_weights():
            nc.vector.quantize_mx(
                out=wcodes[:].rearrange("p a o -> p (a o)").bitcast(FP8X4),
                scales=wsc[:].rearrange("p a o -> p (a o)"),
                in_=wgrp[:].rearrange("p a o t -> p (a o t)"),
            )

        def rows_of(s):
            return slice(P * FIRST[s], P * (FIRST[s] + WIDTHS[s]))

        def load(s):
            if not valid(s):
                return
            w = WIDTHS[s]
            xs = xpool.tile([P, 4, D], BF16, name="xs")
            T["xs", s] = xs
            src = xf[rows_of(s), :].rearrange("(p j) k -> p j k", j=w)
            if s == 0:
                for j in range(w):
                    nc.sync.dma_start(out=xs[:, j, :], in_=src[:, j, :])
            else:
                nc.sync.dma_start(out=xs[:, 0:w, :], in_=src)

        def stats(s):
            if not valid(s):
                return
            w = WIDTHS[s]
            xs = T["xs", s]
            mv = small.tile([P, 4, 2], F32, name="mv")
            T["mv", s] = mv
            for j in range(w):
                for c in range(2):
                    nc.vector.bn_stats(
                        out=sts[s % 4][:, j, 6 * c : 6 * (c + 1)], in_=xs[:, j, 512 * c : 512 * (c + 1)]
                    )
                if j > 0:
                    aggr(s, j - 1)

        def aggr(s, j):
            nc.vector.bn_aggr(out=T["mv", s][:, j, :], in_=sts[s % 4][:, j, :])

        def agl(s):
            if valid(s):
                aggr(s, WIDTHS[s] - 1)

        def early(s):
            if s in EARLY:
                agl(s)
                rstd_stage(s)
                gate(s)
                nmr_stage(s)

        def gate(s):
            if not valid(s):
                return
            w = WIDTHS[s]
            negmu = small.tile([P, 4], F32, name="negmu")
            nc.vector.tensor_scalar_mul(out=negmu[:, 0:w], in0=T["mv", s][:, 0:w, 0], scalar1=-1.0)
            T["negmu", s] = negmu

        def rstd_stage(s):
            if not valid(s):
                return
            w = WIDTHS[s]
            rstd = small.tile([P, 4], F32, name="rstd")
            nc.gpsimd.tensor_tensor(out=rstd[:, 0:w], in0=T["mv", s][:, 0:w, 1], in1=mhalf[:, 0:w], op=ALU.pow)
            T["rstd", s] = rstd

        def nmr_stage(s):
            if not valid(s) or not ("s" in owners(s) or "h" in owners(s)):
                return
            w = WIDTHS[s]
            nmr = small.tile([P, 4], F32, name="nmr")
            if NMR == "s":
                for j in range(w):
                    if owners(s)[j] in "sh":
                        nc.scalar.activation(
                            out=nmr[:, j : j + 1], in_=T["negmu", s][:, j : j + 1], func=ACT.Copy,
                            scale=T["rstd", s][:, j : j + 1],
                        )
            elif NMR == "v":
                nc.vector.tensor_tensor(
                    out=nmr[:, 0:w], in0=T["negmu", s][:, 0:w], in1=T["rstd", s][:, 0:w], op=ALU.mult
                )
            else:
                nc.gpsimd.tensor_tensor(
                    out=nmr[:, 0:w], in0=T["negmu", s][:, 0:w], in1=T["rstd", s][:, 0:w], op=ALU.mult
                )
            T["nmr", s] = nmr

        def norm(s, eng):
            if not valid(s):
                return
            if ("y", s) not in T:
                T["y", s] = ypool.tile([P, 4, D], F32, name="y")
            y = T["y", s]
            xs = T["xs", s]
            rstd = T["rstd", s]
            for j in range(WIDTHS[s]):
                who = owners(s)[j]
                t0, t1_ = 0, 4
                if who == "h":
                    t0, t1_ = (0, G_T) if eng == "g" else (G_T, 4)
                    if eng == "v":
                        continue
                elif who != eng:
                    continue
                y_j = y[:, j, 256 * t0 : 256 * t1_].rearrange("p (t m r) -> p t m r", t=t1_ - t0, r=8)
                x_j = xs[:, j, :].rearrange("p (m t r) -> p t m r", t=4, r=8)[:, t0:t1_, :, :]
                if eng == "s":
                    nc.scalar.activation(
                        out=y_j, in_=x_j, func=ACT.Identity,
                        bias=T["nmr", s][:, j : j + 1], scale=rstd[:, j : j + 1],
                    )
                else:
                    e = nc.gpsimd if eng == "g" else nc.vector
                    if eng == "g":
                        y_j = y[:, j, :].rearrange("p (t m r) -> p m t r", t=4, r=8)
                        x_j = xs[:, j, :].rearrange("p (m t r) -> p m t r", t=4, r=8)
                    e.tensor_scalar(
                        out=y_j, in0=x_j,
                        scalar1=T["negmu", s][:, j : j + 1], scalar2=rstd[:, j : j + 1],
                        op0=ALU.add, op1=ALU.mult,
                    )

        def t1(s, kbs):
            if not valid(s):
                return
            w = WIDTHS[s]
            n = P * w
            y = T["y", s]
            if ("u", s) not in T:
                T["u", s] = upool.tile([P, KB, 512], BF16, name="u")
            u = T["u", s]
            for kb in kbs:
                tp = ps_in.tile([P, 512], F32, tag="tin", name="tp")
                c0 = 256 * (kb % 4) + P * (kb // 4)
                for j in range(w):
                    nc.tensor.transpose(tp[:, P * j : P * (j + 1)], y[:, j, c0 : c0 + P], ident[:])
                if kb in vector_blocks(s):
                    nc.vector.tensor_scalar(
                        out=u[:, kb, 0:n], in0=tp[:, 0:n], scalar1=cols[:, kb : kb + 1],
                        scalar2=cols[:, 8 + kb : 9 + kb], op0=ALU.mult, op1=ALU.add,
                    )
                else:
                    nc.scalar.activation(
                        out=u[:, kb, 0:n], in_=tp[:, 0:n], func=ACT.Identity,
                        bias=cols[:, 8 + kb : 9 + kb], scale=cols[:, kb : kb + 1],
                    )

        def regroup(s):
            if not valid(s):
                return
            n = P * WIDTHS[s]
            grp = gpool.tile([P, 4096], BF16, name="grp", align_bytes=64)
            T["grp", s] = grp
            copy = nc.scalar.copy if s < RG_S else nc.vector.tensor_copy
            copy(
                out=grp[:, 0 : 8 * n].rearrange("p (g c i t) -> p g c t i", g=2, i=4, t=4),
                in_=T["u", s][:, :, 0:n].rearrange("p (g t) (c i) -> p g c t i", g=2, i=4),
            )

        def quant(s):
            if not valid(s):
                return
            n = P * WIDTHS[s]
            codes = cpool.tile([P, 1024], U32, name="codes", align_bytes=64)
            sc = cpool.tile([P, 1024], U8, name="sc", align_bytes=64)
            T["codes", s] = [codes[:, n * g : n * (g + 1)].bitcast(FP8X4) for g in range(2)]
            T["sc", s] = [sc[:, n * g : n * (g + 1)] for g in range(2)]
            nc.vector.quantize_mx(
                out=codes[:, 0 : 2 * n].bitcast(FP8X4), scales=sc[:, 0 : 2 * n], in_=T["grp", s][:, 0 : 8 * n]
            )

        def mx(s, h):
            if not valid(s):
                return
            n = P * WIDTHS[s]
            codes = T["codes", s]
            sc = T["sc", s]
            acc = ps_acc.tile([P, 512], F32, name="acc%d" % h)
            T["acc%d" % h, s] = acc
            for g in range(2):
                nc.tensor.matmul_mx(
                    out=acc[:, 0:n],
                    lhsT=wcodes[:, 2 * h + g, :].bitcast(FP8X4),
                    lhsT_scale=wsc[:, 2 * h + g, :],
                    rhs=codes[g],
                    rhs_scale=sc[g],
                    start=(g == 0),
                    stop=(g == 1),
                )

        def silu(s, h):
            if not valid(s):
                return
            n = P * WIDTHS[s]
            nm = ("hg", "z")[h]
            t = epool.tile([P, 512], F32, name=nm + "T")
            nc.scalar.activation(
                out=t[:, 0:n], in_=T["acc%d" % h, s][:, 0:n], func=ACT.Silu, bias=cols[:, 16 + h : 17 + h], scale=1.0
            )
            T[nm, s] = t

        def qk(s, i, eng):
            if not valid(s) or qk_engine(s)[i] != eng:
                return
            n = P * WIDTHS[s]
            nm = "qk"[i]
            t = epool.tile([P, 512], F32, name=nm + "T")
            gam = cols[:, 18 + i : 19 + i]
            bet = cols[:, 20 + i : 21 + i]
            if eng == "v":
                nc.vector.tensor_scalar(
                    out=t[:, 0:n], in0=T["z", s][:, 0:n], scalar1=gam, scalar2=bet, op0=ALU.mult, op1=ALU.add
                )
            else:
                nc.scalar.activation(out=t[:, 0:n], in_=T["z", s][:, 0:n], func=ACT.Identity, bias=bet, scale=gam)
            T[nm, s] = t

        def t2(s, nm):
            if not valid(s):
                return
            src = T[nm, s]
            to = ps_out.tile([P, 512], F32, tag="tout", name="to_" + nm)
            T["to_" + nm, s] = to
            for j in range(WIDTHS[s]):
                piece = src[:, P * j : P * (j + 1)]
                if nm in COUNTED:
                    nc.tensor.matmul(to[:, P * j : P * (j + 1)], lhsT=piece, rhs=ident[:], start=True, stop=True)
                else:
                    nc.tensor.transpose(to[:, P * j : P * (j + 1)], piece, ident[:])

        def evac(s, nm):
            if not valid(s):
                return
            copy = nc.vector.tensor_copy if nm in vector_outputs(s) else nc.scalar.copy
            w = WIDTHS[s]
            to = T["to_" + nm, s]
            rows = rows_of(s)
            if nm == "hg":
                dst = opool.tile([P, 2, 4, 64], F32, name="o_hg")
                copy(
                    out=dst[:, :, 0:w, :], in_=to[:, 0 : P * w].rearrange("p (j h o) -> p h j o", j=w, h=2)
                )
                for h, name in enumerate("vg"):
                    nc.sync.dma_start(
                        out=outs[name][rows, :].rearrange("(p j) o -> p j o", j=w), in_=dst[:, h, 0:w, :]
                    )
            else:
                dst = opool.tile([P, 512], F32, name="o_" + nm)
                copy(out=dst[:, 0 : P * w], in_=to[:, 0 : P * w])
                nc.sync.dma_start(
                    out=outs[nm][rows, :].rearrange("(p j) o -> p (j o)", j=w), in_=dst[:, 0 : P * w]
                )

        load(0)
        load_consts()
        load(1)
        load_weights()
        for s in range(2, AHEAD):
            load(s)
        stats(0)
        prep_consts()
        prep_weights()
        for i in range(-NL, NS + 3):
            if i + AHEAD >= AHEAD:
                load(i + AHEAD)
            qk(i-2,0,"v")
            agl(i+1)
            rstd_stage(i+1)
            qk(i-2,1,"v")
            regroup(i-1)
            quant(i-1)
            t1(i,(0,1))
            t2(i-2,"hg")
            evac(i-3,"k")
            t1(i,(2,3))
            t2(i-2,"q")
            evac(i-2,"hg")
            gate(i+1)
            t1(i,(4,5))
            t2(i-2,"k")
            nmr_stage(i+1)
            evac(i-2,"q")
            if i == 0:
                quant_weights()
            stats(i+2)
            norm(i+1,"g")
            norm(i+1,"v")
            norm(i+1,"s")
            t1(i,(6,7))
            mx(i-1,1)
            mx(i-1,0)
            silu(i-1,1)
            qk(i-1,0,"s")
            qk(i-1,1,"s")
            silu(i-1,0)
